import numpy as np
import ml_dtypes


def mxq(x, axis, fmt="e4m3"):
    dtype, down = {"e4m3": (ml_dtypes.float8_e4m3fn, 7), "e5m2": (ml_dtypes.float8_e5m2, 14)}[fmt]
    v = np.moveaxis(np.asarray(x, np.float32).astype(ml_dtypes.bfloat16).astype(np.float64), axis, -1)
    blocks = v.reshape(v.shape[:-1] + (-1, 32))
    amax = np.abs(blocks).max(-1, keepdims=True)
    byte = np.maximum(np.where(amax > 0, np.frexp(amax)[1] - 1 + 127, 0) - down, 1)
    scale = np.exp2(byte - 127.0)
    codes = (blocks / scale).astype(np.float32).astype(dtype).astype(np.float64)
    return np.moveaxis((codes * scale).reshape(v.shape), -1, axis)


WIDE = False


def mx_kscale(k):
    if not WIDE:
        return np.ones(k)
    levels = np.array([10, -10, 5, -5, 0])
    a = np.random.permutation(np.resize(levels, k // 512 * 4)).reshape(k // 512, 4)
    idx = np.arange(k)
    return np.exp2(a[idx // 512, idx % 128 // 32])


BF16 = ml_dtypes.bfloat16


def bf(x):
    return np.asarray(x, np.float32).astype(BF16)


def f64(x):
    return np.asarray(x).astype(np.float64)


B, S, IN_F, OUT_F, GS = 4, 2048, 512, 512, 128
GPR = IN_F // GS
N_GROUPS = OUT_F * GPR


def group_kscale():
    u = np.unique(mx_kscale(IN_F))
    u = u[np.argsort(-np.abs(np.log2(u)), kind="stable")]
    return u[np.arange(GPR) % len(u)]


def setup_inputs():
    tg = group_kscale()
    s = np.repeat(tg, GS)
    tflat = np.tile(tg, OUT_F)
    lo, hi = 0.64 / np.sqrt(IN_F), 3.2 / np.sqrt(IN_F)
    x = np.random.standard_normal((B, S, IN_F)) * s
    raw = np.random.standard_normal((OUT_F, IN_F))
    signs = np.where(raw >= 0, 1.0, -1.0)
    scale_pos = np.random.uniform(lo, hi, N_GROUPS) / tflat
    scale_neg = np.random.uniform(lo, hi, N_GROUPS) / tflat
    return {"x": bf(x), "signs": bf(signs), "scale_pos": bf(scale_pos), "scale_neg": bf(scale_neg), "gs": GS}


def reference(x, signs, scale_pos, scale_neg, gs):
    signs = f64(signs)
    out_f, in_f = signs.shape
    sp = np.repeat(f64(scale_pos), gs).reshape(out_f, in_f)
    sn = np.repeat(f64(scale_neg), gs).reshape(out_f, in_f)
    eff_scale = np.where(signs > 0, sp, sn)
    weight = signs * eff_scale
    return mxq(f64(x), 2, "e4m3") @ mxq(weight, 1, "e4m3").T

@@ -1,0 +1,225 @@
+from contextlib import ExitStack
+
+import concourse.mybir as mybir
+from concourse.masks import make_identity
+
+F32 = mybir.dt.float32
+BF16 = mybir.dt.bfloat16
+U32 = mybir.dt.uint32
+U8 = mybir.dt.uint8
+FP8X4 = mybir.dt.float8_e4m3fn_x4
+ALU = mybir.AluOpType
+
+P = 128
+TOKENS = 4 * 2048
+IN_F = 512
+OUT_F = 512
+SLOTS = TOKENS // P
+ROUND = 4
+ROUNDS = SLOTS // ROUND
+LOAD_SLOTS = [4,4,4,4,8,8,16,16]
+STORE_SLOTS = [8,8,8,8,8,8,8,8]
+AHEAD = 5
+PIN = True
+
+FLOPS = 2 * TOKENS * IN_F * OUT_F
+
+
+def tile_signcondpackedbitlinear_t_kernel(tc, x, signs, scale_pos, scale_neg, gs, out):
+    nc = tc.nc
+    assert gs == 128
+    groups = IN_F // gs
+    o_tiles = OUT_F // P
+    x_rows = x.flatten_outer_dims().rearrange("(p j) k -> p j k", p=P)
+    out_rows = out.flatten_outer_dims().rearrange("(p j) o -> p j o", p=P)
+
+    with ExitStack() as ctx:
+        keep = ctx.enter_context(tc.tile_pool(name="keep", bufs=1))
+        stage = ctx.enter_context(tc.tile_pool(name="stage", bufs=3))
+        quant = ctx.enter_context(tc.tile_pool(name="quant", bufs=AHEAD + 2))
+        outs = ctx.enter_context(tc.tile_pool(name="outs", bufs=5))
+        psum_t = ctx.enter_context(tc.psum_pool(name="psum_t", bufs=4))
+        psum_o = ctx.enter_context(tc.psum_pool(name="psum_o", bufs=4))
+        if PIN:
+            ctx.enter_context(tc.manual_schedule())
+
+        sp_sb = keep.tile([P, o_tiles * groups], BF16, name="sp_sb")
+        sn_sb = keep.tile([P, o_tiles * groups], BF16, name="sn_sb")
+        nc.scalar.dma_start(out=sp_sb[:], in_=scale_pos.rearrange("(p c) -> p c", p=P))
+        nc.scalar.dma_start(out=sn_sb[:], in_=scale_neg.rearrange("(p c) -> p c", p=P))
+        signs_sb = keep.tile([P, o_tiles * IN_F], BF16, name="signs_sb")
+        nc.sync.dma_start(out=signs_sb[:], in_=signs.rearrange("(p t) i -> p (t i)", t=o_tiles))
+
+        x_words = []
+        first = 0
+        for n, slots in enumerate(LOAD_SLOTS):
+            x_sb = keep.tile([P, slots * IN_F], BF16, name="x_sb%d" % n)
+            nc.sync.dma_start(
+                out=x_sb[:],
+                in_=x_rows[:, first : first + slots, :].rearrange("p j k -> p (j k)"),
+            )
+            words = x_sb[:].bitcast(F32).rearrange("p (j q u) -> p j q u", q=P, u=2)
+            for j in range(slots):
+                x_words.append(words[:, j, :, :])
+            first += slots
+
+        ident = keep.tile([P, P], F32, name="ident")
+        make_identity(nc, ident[:])
+
+        banks_of = {}
+        grouped_of = {}
+        codes_of = {}
+        scales_of = {}
+        acc_of = {}
+
+        def copy_on(engine, dst, src):
+            if engine == "v":
+                nc.vector.tensor_copy(out=dst, in_=src)
+            else:
+                nc.scalar.copy(out=dst, in_=src)
+
+        def transposes(r):
+            banks_of[r] = []
+            for b in range(2):
+                xt = psum_t.tile([P, 2, 2 * P], F32, name="xt")
+                banks_of[r].append(xt)
+                for a in range(2):
+                    src = x_words[ROUND * r + 2 * b + a]
+                    for u in range(2):
+                        nc.tensor.transpose(xt[:, u, a * P : (a + 1) * P], src[:, :, u], ident[:])
+
+        def regroup(r, engines):
+            grouped = stage.tile([P, ROUND * P * 4], BF16, name="grouped", align_bytes=64)
+            grouped_of[r] = grouped
+            g32 = grouped[:].bitcast(F32).rearrange("p (c u) -> p c u", u=2)
+            for b in range(2):
+                copy_on(
+                    engines[b],
+                    g32[:, b * 2 * P : (b + 1) * 2 * P, :],
+                    banks_of[r][b][:].rearrange("p u c -> p c u"),
+                )
+
+        def quantise(r):
+            codes = quant.tile([P, ROUND * P], U32, name="codes", align_bytes=64)
+            scl = quant.tile([P, ROUND * P], U8, name="scl", align_bytes=64)
+            codes_of[r] = codes
+            scales_of[r] = scl
+            nc.vector.quantize_mx(out=codes[:].bitcast(FP8X4), scales=scl[:], in_=grouped_of[r][:])
+
+        half = o_tiles * groups // 2
+        shape = [P, half, gs]
+        s3 = signs_sb[:].rearrange("p (c i) -> p c i", i=gs)
+        w_sb = keep.tile([P, o_tiles * IN_F], BF16, name="w_sb")
+        w3 = w_sb[:].rearrange("p (c i) -> p c i", i=gs)
+        w_words = w_sb[:].bitcast(F32).rearrange("p (t q u) -> p t q u", q=P, u=2)
+        w_grouped = keep.tile([P, OUT_F * 4], BF16, name="w_grouped", align_bytes=64)
+        wg32 = w_grouped[:].bitcast(F32).rearrange("q (p t u) -> q p t u", t=o_tiles, u=2)
+        w_codes = keep.tile([P, OUT_F], U32, name="w_codes", align_bytes=64)
+        w_scl = keep.tile([P, OUT_F], U8, name="w_scl", align_bytes=64)
+
+        def build(h):
+            cs = slice(h * half, (h + 1) * half)
+            pos = keep.tile(shape, BF16, name="pos%d" % h)
+            neg = keep.tile(shape, BF16, name="neg%d" % h)
+            nc.vector.scalar_tensor_tensor(
+                out=pos[:], in0=s3[:, cs, :], scalar=0.0,
+                in1=sp_sb[:, cs].unsqueeze(2).to_broadcast(shape), op0=ALU.max, op1=ALU.mult,
+            )
+            nc.vector.scalar_tensor_tensor(
+                out=neg[:], in0=s3[:, cs, :], scalar=0.0,
+                in1=sn_sb[:, cs].unsqueeze(2).to_broadcast(shape), op0=ALU.min, op1=ALU.mult,
+            )
+            nc.vector.tensor_tensor(out=w3[:, cs, :], in0=pos[:], in1=neg[:], op=ALU.add)
+
+        def w_transposes(b, engine):
+            wt = psum_t.tile([P, 2, 2 * P], F32, name="xt")
+            for a in range(2):
+                for u in range(2):
+                    nc.tensor.transpose(
+                        wt[:, u, a * P : (a + 1) * P], w_words[:, 2 * b + a, :, u], ident[:]
+                    )
+            copy_on(
+                engine,
+                wg32[:, :, 2 * b : 2 * b + 2, :],
+                wt[:].rearrange("q u (a p) -> q p a u", a=2),
+            )
+
+        def passes(r):
+            acc_of[r] = []
+            for a in range(ROUND):
+                acc = psum_o.tile([P, OUT_F], F32, name="acc")
+                acc_of[r].append(acc)
+                nc.tensor.matmul_mx(
+                    out=acc[:],
+                    lhsT=codes_of[r][:, a * P : (a + 1) * P].bitcast(FP8X4),
+                    lhsT_scale=scales_of[r][:, a * P : (a + 1) * P],
+                    rhs=w_codes[:].bitcast(FP8X4),
+                    rhs_scale=w_scl[:],
+                    start=True,
+                    stop=True,
+                )
+
+        store_start = {}
+        store_end = {}
+        first = 0
+        for slots in STORE_SLOTS:
+            store_start[first] = slots
+            store_end[first + slots - 1] = first
+            first += slots
+        live = {}
+
+        def drain(r, a, engine):
+            j = ROUND * r + a
+            if j in store_start:
+                out_sb = outs.tile([P, max(STORE_SLOTS) * OUT_F], F32, name="out_sb")
+                live["tile"] = out_sb
+                live["first"] = j
+            k = j - live["first"]
+            copy_on(engine, live["tile"][:, k * OUT_F : (k + 1) * OUT_F], acc_of[r][a][:])
+
+        def store(r):
+            j = ROUND * r + ROUND - 1
+            if j in store_end:
+                f = store_end[j]
+                nc.sync.dma_start(
+                    out=out_rows[:, f : j + 1, :].rearrange("p j o -> p (j o)"),
+                    in_=live["tile"][:, : (j + 1 - f) * OUT_F],
+                )
+
+        transposes(0)
+        regroup(0, "ss")
+        build(0)
+        transposes(1)
+        regroup(1, "ss")
+        build(1)
+        transposes(2)
+        regroup(2, "ss")
+        w_transposes(0, "s")
+        quantise(0)
+        transposes(3)
+        regroup(3, "ss")
+        w_transposes(1, "s")
+        quantise(1)
+        nc.vector.quantize_mx(out=w_codes[:].bitcast(FP8X4), scales=w_scl[:], in_=w_grouped[:])
+        for r in range(4, AHEAD):
+            transposes(r)
+            regroup(r, "ss")
+        for r in range(2, AHEAD - 1):
+            quantise(r)
+
+        for s in range(ROUNDS):
+            passes(s)
+            busy = s + AHEAD < ROUNDS
+            if busy:
+                transposes(s + AHEAD)
+            if s + AHEAD - 1 < ROUNDS:
+                quantise(s + AHEAD - 1)
+            if busy:
+                share = "svss" if s % 2 == 1 else "ssss"
+            else:
+                share = "svsv"
+            for a in range(ROUND):
+                drain(s, a, share[a])
+            store(s)
+            if busy:
+                regroup(s + AHEAD, "vv")

@@ -18,7 +18,7 @@ SLOTS = TOKENS // P
 ROUND = 4
 ROUNDS = SLOTS // ROUND
 LOAD_SLOTS = [4,4,4,4,8,8,16,16]
-STORE_SLOTS = [8,8,8,8,8,8,8,8]
+STORE_SLOTS = [4,4,4,4,4,4,4,4,4,4,4,4,4,4,4,4]
 AHEAD = 5
 PIN = True
 
@@ -37,7 +37,7 @@ def tile_signcondpackedbitlinear_t_kernel(tc, x, signs, scale_pos, scale_neg, gs
         keep = ctx.enter_context(tc.tile_pool(name="keep", bufs=1))
         stage = ctx.enter_context(tc.tile_pool(name="stage", bufs=3))
         quant = ctx.enter_context(tc.tile_pool(name="quant", bufs=AHEAD + 2))
-        outs = ctx.enter_context(tc.tile_pool(name="outs", bufs=5))
+        outs = ctx.enter_context(tc.tile_pool(name="outs", bufs=10))
         psum_t = ctx.enter_context(tc.psum_pool(name="psum_t", bufs=4))
         psum_o = ctx.enter_context(tc.psum_pool(name="psum_o", bufs=4))
         if PIN:

@@ -18,7 +18,7 @@ SLOTS = TOKENS // P
 ROUND = 4
 ROUNDS = SLOTS // ROUND
 LOAD_SLOTS = [4,4,4,4,8,8,16,16]
-STORE_SLOTS = [4,4,4,4,4,4,4,4,4,4,4,4,4,4,4,4]
+STORE_SLOTS = [8,8,8,8,8,8,4,4,4,4]
 AHEAD = 5
 PIN = True
 
@@ -37,7 +37,7 @@ def tile_signcondpackedbitlinear_t_kernel(tc, x, signs, scale_pos, scale_neg, gs
         keep = ctx.enter_context(tc.tile_pool(name="keep", bufs=1))
         stage = ctx.enter_context(tc.tile_pool(name="stage", bufs=3))
         quant = ctx.enter_context(tc.tile_pool(name="quant", bufs=AHEAD + 2))
-        outs = ctx.enter_context(tc.tile_pool(name="outs", bufs=10))
+        outs = ctx.enter_context(tc.tile_pool(name="outs", bufs=5))
         psum_t = ctx.enter_context(tc.psum_pool(name="psum_t", bufs=4))
         psum_o = ctx.enter_context(tc.psum_pool(name="psum_o", bufs=4))
         if PIN:

@@ -18,9 +18,9 @@ SLOTS = TOKENS // P
 ROUND = 4
 ROUNDS = SLOTS // ROUND
 LOAD_SLOTS = [4,4,4,4,8,8,16,16]
-STORE_SLOTS = [8,8,8,8,8,8,4,4,4,4]
+STORE_SLOTS = [4,4,4,4,4,4,4,4,4,4,4,4,4,4,4,4]
 AHEAD = 5
-PIN = True
+PIN = False
 
 FLOPS = 2 * TOKENS * IN_F * OUT_F
 
@@ -37,7 +37,7 @@ def tile_signcondpackedbitlinear_t_kernel(tc, x, signs, scale_pos, scale_neg, gs
         keep = ctx.enter_context(tc.tile_pool(name="keep", bufs=1))
         stage = ctx.enter_context(tc.tile_pool(name="stage", bufs=3))
         quant = ctx.enter_context(tc.tile_pool(name="quant", bufs=AHEAD + 2))
-        outs = ctx.enter_context(tc.tile_pool(name="outs", bufs=5))
+        outs = ctx.enter_context(tc.tile_pool(name="outs", bufs=10))
         psum_t = ctx.enter_context(tc.psum_pool(name="psum_t", bufs=4))
         psum_o = ctx.enter_context(tc.psum_pool(name="psum_o", bufs=4))
         if PIN:

@@ -18,7 +18,7 @@ SLOTS = TOKENS // P
 ROUND = 4
 ROUNDS = SLOTS // ROUND
 LOAD_SLOTS = [4,4,4,4,8,8,16,16]
-STORE_SLOTS = [4,4,4,4,4,4,4,4,4,4,4,4,4,4,4,4]
+STORE_SLOTS = [8,8,8,8,8,8,8,4,4]
 AHEAD = 5
 PIN = False
 
@@ -37,7 +37,7 @@ def tile_signcondpackedbitlinear_t_kernel(tc, x, signs, scale_pos, scale_neg, gs
         keep = ctx.enter_context(tc.tile_pool(name="keep", bufs=1))
         stage = ctx.enter_context(tc.tile_pool(name="stage", bufs=3))
         quant = ctx.enter_context(tc.tile_pool(name="quant", bufs=AHEAD + 2))
-        outs = ctx.enter_context(tc.tile_pool(name="outs", bufs=10))
+        outs = ctx.enter_context(tc.tile_pool(name="outs", bufs=7))
         psum_t = ctx.enter_context(tc.psum_pool(name="psum_t", bufs=4))
         psum_o = ctx.enter_context(tc.psum_pool(name="psum_o", bufs=4))
         if PIN:

@@ -18,7 +18,7 @@ SLOTS = TOKENS // P
 ROUND = 4
 ROUNDS = SLOTS // ROUND
 LOAD_SLOTS = [4,4,4,4,8,8,16,16]
-STORE_SLOTS = [8,8,8,8,8,8,8,4,4]
+STORE_SLOTS = [8,8,8,8,8,8,8,4,2,1,1]
 AHEAD = 5
 PIN = False
 
@@ -177,8 +177,7 @@ def tile_signcondpackedbitlinear_t_kernel(tc, x, signs, scale_pos, scale_neg, gs
             k = j - live["first"]
             copy_on(engine, live["tile"][:, k * OUT_F : (k + 1) * OUT_F], acc_of[r][a][:])
 
-        def store(r):
-            j = ROUND * r + ROUND - 1
+        def store(j):
             if j in store_end:
                 f = store_end[j]
                 nc.sync.dma_start(
@@ -220,6 +219,6 @@ def tile_signcondpackedbitlinear_t_kernel(tc, x, signs, scale_pos, scale_neg, gs
                 share = "svsv"
             for a in range(ROUND):
                 drain(s, a, share[a])
-            store(s)
+                store(ROUND * s + a)
             if busy:
                 regroup(s + AHEAD, "vv")

from contextlib import ExitStack

import concourse.mybir as mybir
from concourse.masks import make_identity

F32 = mybir.dt.float32
BF16 = mybir.dt.bfloat16
U32 = mybir.dt.uint32
U8 = mybir.dt.uint8
FP8X4 = mybir.dt.float8_e4m3fn_x4
ALU = mybir.AluOpType

P = 128
TOKENS = 4 * 2048
IN_F = 512
OUT_F = 512
SLOTS = TOKENS // P
ROUND = 4
ROUNDS = SLOTS // ROUND
LOAD_SLOTS = [4,4,4,4,8,8,16,16]
STORE_SLOTS = [8,8,8,8,8,8,8,4,2,1,1]
AHEAD = 5
PIN = False

FLOPS = 2 * TOKENS * IN_F * OUT_F


def tile_signcondpackedbitlinear_t_kernel(tc, x, signs, scale_pos, scale_neg, gs, out):
    nc = tc.nc
    assert gs == 128
    groups = IN_F // gs
    o_tiles = OUT_F // P
    x_rows = x.flatten_outer_dims().rearrange("(p j) k -> p j k", p=P)
    out_rows = out.flatten_outer_dims().rearrange("(p j) o -> p j o", p=P)

    with ExitStack() as ctx:
        keep = ctx.enter_context(tc.tile_pool(name="keep", bufs=1))
        stage = ctx.enter_context(tc.tile_pool(name="stage", bufs=3))
        quant = ctx.enter_context(tc.tile_pool(name="quant", bufs=AHEAD + 2))
        outs = ctx.enter_context(tc.tile_pool(name="outs", bufs=7))
        psum_t = ctx.enter_context(tc.psum_pool(name="psum_t", bufs=4))
        psum_o = ctx.enter_context(tc.psum_pool(name="psum_o", bufs=4))
        if PIN:
            ctx.enter_context(tc.manual_schedule())

        sp_sb = keep.tile([P, o_tiles * groups], BF16, name="sp_sb")
        sn_sb = keep.tile([P, o_tiles * groups], BF16, name="sn_sb")
        nc.scalar.dma_start(out=sp_sb[:], in_=scale_pos.rearrange("(p c) -> p c", p=P))
        nc.scalar.dma_start(out=sn_sb[:], in_=scale_neg.rearrange("(p c) -> p c", p=P))
        signs_sb = keep.tile([P, o_tiles * IN_F], BF16, name="signs_sb")
        nc.sync.dma_start(out=signs_sb[:], in_=signs.rearrange("(p t) i -> p (t i)", t=o_tiles))

        x_words = []
        first = 0
        for n, slots in enumerate(LOAD_SLOTS):
            x_sb = keep.tile([P, slots * IN_F], BF16, name="x_sb%d" % n)
            nc.sync.dma_start(
                out=x_sb[:],
                in_=x_rows[:, first : first + slots, :].rearrange("p j k -> p (j k)"),
            )
            words = x_sb[:].bitcast(F32).rearrange("p (j q u) -> p j q u", q=P, u=2)
            for j in range(slots):
                x_words.append(words[:, j, :, :])
            first += slots

        ident = keep.tile([P, P], F32, name="ident")
        make_identity(nc, ident[:])

        banks_of = {}
        grouped_of = {}
        codes_of = {}
        scales_of = {}
        acc_of = {}

        def copy_on(engine, dst, src):
            if engine == "v":
                nc.vector.tensor_copy(out=dst, in_=src)
            else:
                nc.scalar.copy(out=dst, in_=src)

        def transposes(r):
            banks_of[r] = []
            for b in range(2):
                xt = psum_t.tile([P, 2, 2 * P], F32, name="xt")
                banks_of[r].append(xt)
                for a in range(2):
                    src = x_words[ROUND * r + 2 * b + a]
                    for u in range(2):
                        nc.tensor.transpose(xt[:, u, a * P : (a + 1) * P], src[:, :, u], ident[:])

        def regroup(r, engines):
            grouped = stage.tile([P, ROUND * P * 4], BF16, name="grouped", align_bytes=64)
            grouped_of[r] = grouped
            g32 = grouped[:].bitcast(F32).rearrange("p (c u) -> p c u", u=2)
            for b in range(2):
                copy_on(
                    engines[b],
                    g32[:, b * 2 * P : (b + 1) * 2 * P, :],
                    banks_of[r][b][:].rearrange("p u c -> p c u"),
                )

        def quantise(r):
            codes = quant.tile([P, ROUND * P], U32, name="codes", align_bytes=64)
            scl = quant.tile([P, ROUND * P], U8, name="scl", align_bytes=64)
            codes_of[r] = codes
            scales_of[r] = scl
            nc.vector.quantize_mx(out=codes[:].bitcast(FP8X4), scales=scl[:], in_=grouped_of[r][:])

        half = o_tiles * groups // 2
        shape = [P, half, gs]
        s3 = signs_sb[:].rearrange("p (c i) -> p c i", i=gs)
        w_sb = keep.tile([P, o_tiles * IN_F], BF16, name="w_sb")
        w3 = w_sb[:].rearrange("p (c i) -> p c i", i=gs)
        w_words = w_sb[:].bitcast(F32).rearrange("p (t q u) -> p t q u", q=P, u=2)
        w_grouped = keep.tile([P, OUT_F * 4], BF16, name="w_grouped", align_bytes=64)
        wg32 = w_grouped[:].bitcast(F32).rearrange("q (p t u) -> q p t u", t=o_tiles, u=2)
        w_codes = keep.tile([P, OUT_F], U32, name="w_codes", align_bytes=64)
        w_scl = keep.tile([P, OUT_F], U8, name="w_scl", align_bytes=64)

        def build(h):
            cs = slice(h * half, (h + 1) * half)
            pos = keep.tile(shape, BF16, name="pos%d" % h)
            neg = keep.tile(shape, BF16, name="neg%d" % h)
            nc.vector.scalar_tensor_tensor(
                out=pos[:], in0=s3[:, cs, :], scalar=0.0,
                in1=sp_sb[:, cs].unsqueeze(2).to_broadcast(shape), op0=ALU.max, op1=ALU.mult,
            )
            nc.vector.scalar_tensor_tensor(
                out=neg[:], in0=s3[:, cs, :], scalar=0.0,
                in1=sn_sb[:, cs].unsqueeze(2).to_broadcast(shape), op0=ALU.min, op1=ALU.mult,
            )
            nc.vector.tensor_tensor(out=w3[:, cs, :], in0=pos[:], in1=neg[:], op=ALU.add)

        def w_transposes(b, engine):
            wt = psum_t.tile([P, 2, 2 * P], F32, name="xt")
            for a in range(2):
                for u in range(2):
                    nc.tensor.transpose(
                        wt[:, u, a * P : (a + 1) * P], w_words[:, 2 * b + a, :, u], ident[:]
                    )
            copy_on(
                engine,
                wg32[:, :, 2 * b : 2 * b + 2, :],
                wt[:].rearrange("q u (a p) -> q p a u", a=2),
            )

        def passes(r):
            acc_of[r] = []
            for a in range(ROUND):
                acc = psum_o.tile([P, OUT_F], F32, name="acc")
                acc_of[r].append(acc)
                nc.tensor.matmul_mx(
                    out=acc[:],
                    lhsT=codes_of[r][:, a * P : (a + 1) * P].bitcast(FP8X4),
                    lhsT_scale=scales_of[r][:, a * P : (a + 1) * P],
                    rhs=w_codes[:].bitcast(FP8X4),
                    rhs_scale=w_scl[:],
                    start=True,
                    stop=True,
                )

        store_start = {}
        store_end = {}
        first = 0
        for slots in STORE_SLOTS:
            store_start[first] = slots
            store_end[first + slots - 1] = first
            first += slots
        live = {}

        def drain(r, a, engine):
            j = ROUND * r + a
            if j in store_start:
                out_sb = outs.tile([P, max(STORE_SLOTS) * OUT_F], F32, name="out_sb")
                live["tile"] = out_sb
                live["first"] = j
            k = j - live["first"]
            copy_on(engine, live["tile"][:, k * OUT_F : (k + 1) * OUT_F], acc_of[r][a][:])

        def store(j):
            if j in store_end:
                f = store_end[j]
                nc.sync.dma_start(
                    out=out_rows[:, f : j + 1, :].rearrange("p j o -> p (j o)"),
                    in_=live["tile"][:, : (j + 1 - f) * OUT_F],
                )

        transposes(0)
        regroup(0, "ss")
        build(0)
        transposes(1)
        regroup(1, "ss")
        build(1)
        transposes(2)
        regroup(2, "ss")
        w_transposes(0, "s")
        quantise(0)
        transposes(3)
        regroup(3, "ss")
        w_transposes(1, "s")
        quantise(1)
        nc.vector.quantize_mx(out=w_codes[:].bitcast(FP8X4), scales=w_scl[:], in_=w_grouped[:])
        for r in range(4, AHEAD):
            transposes(r)
            regroup(r, "ss")
        for r in range(2, AHEAD - 1):
            quantise(r)

        for s in range(ROUNDS):
            passes(s)
            busy = s + AHEAD < ROUNDS
            if busy:
                transposes(s + AHEAD)
            if s + AHEAD - 1 < ROUNDS:
                quantise(s + AHEAD - 1)
            if busy:
                share = "svss" if s % 2 == 1 else "ssss"
            else:
                share = "svsv"
            for a in range(ROUND):
                drain(s, a, share[a])
                store(ROUND * s + a)
            if busy:
                regroup(s + AHEAD, "vv")
